import numpy as np
import ml_dtypes


def mxq(x, axis, fmt="e4m3"):
    dtype, down = {"e4m3": (ml_dtypes.float8_e4m3fn, 7), "e5m2": (ml_dtypes.float8_e5m2, 14)}[fmt]
    v = np.moveaxis(np.asarray(x, np.float32).astype(ml_dtypes.bfloat16).astype(np.float64), axis, -1)
    blocks = v.reshape(v.shape[:-1] + (-1, 32))
    amax = np.abs(blocks).max(-1, keepdims=True)
    byte = np.maximum(np.where(amax > 0, np.frexp(amax)[1] - 1 + 127, 0) - down, 1)
    scale = np.exp2(byte - 127.0)
    codes = (blocks / scale).astype(np.float32).astype(dtype).astype(np.float64)
    return np.moveaxis((codes * scale).reshape(v.shape), -1, axis)


WIDE = False


def mx_kscale(k):
    if not WIDE:
        return np.ones(k)
    levels = np.array([10, -10, 5, -5, 0])
    a = np.random.permutation(np.resize(levels, k // 512 * 4)).reshape(k // 512, 4)
    idx = np.arange(k)
    return np.exp2(a[idx // 512, idx % 128 // 32])


BF16 = ml_dtypes.bfloat16


def bf(x):
    return np.asarray(x, np.float32).astype(BF16)


def f64(x):
    return np.asarray(x).astype(np.float64)


B, HEADS, CH, H, W, HSP, WSP = 2, 6, 128, 32, 64, 16, 32
C = HEADS * CH
U, V = H // HSP, W // WSP
NW = U * V
N = HSP * WSP


def _vid2win(x):
    x = x.reshape(B, HEADS, CH, U, HSP, V, WSP)
    x = x.transpose(0, 3, 5, 1, 4, 6, 2)
    return x.reshape(B * NW, HEADS, N, CH)


def setup_inputs():
    s = mx_kscale(N)
    sp = np.tile(s.reshape(HSP, WSP), (U, V))
    kv = np.random.standard_normal((2, B, C, H, W))
    kv[1] = kv[1] / sp * s.max()
    q = np.random.standard_normal((B, C, H, W)) * 1.5
    mask = np.random.standard_normal((NW, N, N)) + np.log(s)[None, None, :]
    return {"kv": bf(kv), "q": bf(q), "mask": bf(mask)}


def reference(kv, q, mask):
    kv = f64(kv)
    k, v = kv[0], kv[1]
    qw = _vid2win(f64(q))
    kw = _vid2win(k)
    vw = _vid2win(v)
    attn = (qw @ kw.transpose(0, 1, 3, 2)) * CH ** (-0.5)
    attn = attn.reshape(B, NW, HEADS, N, N) + f64(mask)[None, :, None]
    attn = attn.reshape(B * NW, HEADS, N, N)
    e = np.exp(attn - attn.max(-1, keepdims=True))
    x = (mxq(e, 3, "e4m3") @ mxq(vw, 2, "e4m3")) / e.sum(-1, keepdims=True)
    x = x.reshape(B, U, V, HEADS, HSP, WSP, CH)
    x = x.transpose(0, 3, 6, 1, 4, 2, 5)
    return x.reshape(B, C, H, W)

@@ -1,0 +1,339 @@
+import math
+from contextlib import ExitStack
+
+import concourse.mybir as mybir
+from concourse.masks import make_identity
+
+F32 = mybir.dt.float32
+BF16 = mybir.dt.bfloat16
+U32 = mybir.dt.uint32
+U8 = mybir.dt.uint8
+FP8X4 = mybir.dt.float8_e4m3fn_x4
+AF = mybir.ActivationFunctionType
+ALU = mybir.AluOpType
+AX = mybir.AxisListType
+
+P = 128
+NB, HEADS, NWIN, N = 2, 6, 4, 512
+NBD = NB * HEADS
+NBLK = 2 * NBD
+NUNITS = 2 * NBLK
+HPIX = 1024
+SQRT_CH = math.sqrt(128.0)
+SCALE = 1.0 / SQRT_CH
+FLOPS = NUNITS * 2 * (2 * N * N * P)
+
+MANUAL = True
+NB_ON_POOL = False
+VE_ON_ACT = True
+OE_DVE_EVERY = 4
+
+
+def tile_window_attention_kernel(tc, kv, q, mask, out):
+    nc = tc.nc
+    q_v = q.rearrange("b (d c) (u h) w -> u (b d) c (h w)", c=P, u=2)
+    kv_v = kv.rearrange("s b (d c) (u h) w -> s u (b d) c (h w)", c=P, u=2)
+    out_v = out.rearrange("b (d c) (u h) w -> u (b d) c (h w)", c=P, u=2)
+    mask_v = mask.rearrange("w (j p) k -> w p j k", p=P)
+
+    with ExitStack() as ctx:
+        const = ctx.enter_context(tc.tile_pool(name="const", bufs=1))
+        raw = ctx.enter_context(tc.tile_pool(name="raw", bufs=4))
+        mraw = ctx.enter_context(tc.tile_pool(name="mraw", bufs=4))
+        win = ctx.enter_context(tc.tile_pool(name="win", bufs=3))
+        vq = ctx.enter_context(tc.tile_pool(name="vq", bufs=4))
+        small = ctx.enter_context(tc.tile_pool(name="small", bufs=8))
+        epool = ctx.enter_context(tc.tile_pool(name="epool", bufs=8))
+        gpool = ctx.enter_context(tc.tile_pool(name="gpool", bufs=4))
+        opool = ctx.enter_context(tc.tile_pool(name="opool", bufs=3))
+        ps_s = ctx.enter_context(tc.psum_pool(name="ps_s", bufs=4))
+        ps_t = ctx.enter_context(tc.psum_pool(name="ps_t", bufs=2))
+        ps_o = ctx.enter_context(tc.psum_pool(name="ps_o", bufs=1))
+        if MANUAL:
+            ctx.enter_context(tc.manual_schedule())
+
+        ident_b = const.tile([P, P], BF16, name="ident_b")
+        ident_f = const.tile([P, P], F32, name="ident_f")
+        make_identity(nc, ident_b[:])
+        make_identity(nc, ident_f[:])
+        mask_t = const.tile([P, NWIN, 4, N], F32, name="mask_t")
+
+        blk_t = {}
+        unit = {}
+        chunk = {}
+
+        def load_mask(w):
+            m_sb = mraw.tile([P, 4, N], BF16, name="m_sb")
+            nc.sync.dma_start(out=m_sb[:], in_=mask_v[w])
+            blk_t[("m", w)] = m_sb
+
+        def mask_transposes(w, half):
+            m_sb = blk_t[("m", w)]
+            mt = ps_t.tile([P, 2, N], BF16, name="mt", tag="tr")
+            for ti in range(2):
+                for j in range(4):
+                    t = 2 * half + ti
+                    nc.tensor.transpose(mt[:, ti, j * P:(j + 1) * P], m_sb[:, j, t * P:(t + 1) * P], ident_b[:])
+            blk_t[("mt", w, half)] = mt
+
+        def mask_scale(w, half, on_scalar):
+            dst = mask_t[:, w, 2 * half:2 * half + 2, :]
+            src = blk_t[("mt", w, half)][:]
+            if on_scalar:
+                nc.scalar.mul(out=dst, in_=src, mul=SQRT_CH)
+            else:
+                nc.vector.tensor_scalar_mul(out=dst, in0=src, scalar1=SQRT_CH)
+
+        def load_one(what, blk):
+            uw, bd = blk // NBD, blk % NBD
+            t = raw.tile([P, HPIX], BF16, name=what)
+            src = {"q_raw": q_v[uw, bd], "k_raw": kv_v[0, uw, bd], "v_raw": kv_v[1, uw, bd]}[what]
+            nc.sync.dma_start(out=t[:], in_=src)
+            blk_t[(what, blk)] = t
+
+        def load_blk(blk):
+            for what in ("q_raw", "k_raw", "v_raw"):
+                load_one(what, blk)
+
+        def to_windows(what, blk):
+            dst = win.tile([P, 2, N], BF16, name=what + "_win")
+            nc.vector.tensor_copy(
+                out=dst[:].rearrange("c v (h w) -> c v h w", h=16),
+                in_=blk_t[(what + "_raw", blk)][:].rearrange("c (h v w) -> c v h w", h=16, v=2),
+            )
+            blk_t[(what + "_win", blk)] = dst
+
+        def v_transposes(blk):
+            v_win = blk_t[("v_win", blk)]
+            vt = ps_t.tile([P, 2, 2, P], F32, name="vt", tag="tr")
+            for vw in range(2):
+                for u in range(2):
+                    nc.tensor.transpose(vt[:, vw, u, :], v_win[:, vw, :].bitcast(F32)[:, u * P:(u + 1) * P], ident_f[:])
+            blk_t[("vt", blk)] = vt
+
+        def v_regroup(blk, on_scalar):
+            vg = vq.tile([P, 2, P, 4], BF16, name="vg", align_bytes=64)
+            src = blk_t[("vt", blk)][:].rearrange("p w u c -> p w c u")
+            if on_scalar:
+                nc.scalar.copy(out=vg[:].bitcast(F32), in_=src)
+            else:
+                nc.vector.tensor_copy(out=vg[:].bitcast(F32), in_=src)
+            blk_t[("vg", blk)] = vg
+
+        def quantise_v(blk):
+            v_codes = vq.tile([P, 2 * P], U32, name="v_codes", align_bytes=64)
+            v_scl = vq.tile([P, 2 * P], U8, name="v_scl", align_bytes=64)
+            nc.vector.quantize_mx(
+                out=v_codes[:].bitcast(FP8X4),
+                scales=v_scl[:],
+                in_=blk_t[("vg", blk)][:].rearrange("p w c t -> p (w c t)"),
+            )
+            blk_t[("v_codes", blk)] = v_codes
+            blk_t[("v_scl", blk)] = v_scl
+
+        def scores(n, j, mm_first):
+            blk, vw = n // 2, n % 2
+            w = 2 * (blk // NBD) + vw
+            lhs = blk_t[("q_win", blk)][:, vw, j * P:(j + 1) * P]
+            rhs = blk_t[("k_raw", blk)][:].rearrange("c (h v x) -> c h v x", h=16, v=2)[:, :, vw, :]
+            s_ps = ps_s.tile([P, N], F32, name="s_ps")
+            if mm_first:
+                nc.tensor.matmul(out=s_ps[:], lhsT=lhs, rhs=rhs, start=True, stop=False)
+            for t in range(4):
+                nc.tensor.matmul(
+                    out=s_ps[:, t * P:(t + 1) * P],
+                    lhsT=mask_t[:, w, t, j * P:(j + 1) * P],
+                    rhs=ident_f[:],
+                    is_transpose=True,
+                    start=(t == 0 and not mm_first),
+                    stop=(t == 3 and mm_first),
+                )
+            if not mm_first:
+                nc.tensor.matmul(out=s_ps[:], lhsT=lhs, rhs=rhs, start=False, stop=True)
+            chunk[("s", n, j)] = s_ps
+
+        def row_max(n, half):
+            nm = small.tile([P, 2], F32, name="nm")
+            for i in range(2):
+                nc.vector.tensor_reduce(out=nm[:, i:i + 1], in_=chunk[("s", n, 2 * half + i)][:], axis=AX.X,
+                                        op=ALU.max, negate=True)
+            nb = small.tile([P, 2], F32, name="nb")
+            if NB_ON_POOL:
+                nc.gpsimd.tensor_scalar(out=nb[:], in0=nm[:], scalar1=SCALE, scalar2=0.0, op0=ALU.mult, op1=ALU.add)
+            else:
+                nc.vector.tensor_scalar_mul(out=nb[:], in0=nm[:], scalar1=SCALE)
+            chunk[("nb", n, half)] = nb
+
+        def exps(n, half):
+            if half == 0:
+                unit[("rs", n)] = small.tile([P, 4], F32, name="rs")
+            for i in range(2):
+                j = 2 * half + i
+                e_sb = epool.tile([P, N], BF16, name="e_sb")
+                nc.scalar.activation(
+                    out=e_sb[:],
+                    in_=chunk[("s", n, j)][:],
+                    func=AF.Exp,
+                    bias=chunk[("nb", n, half)][:, i:i + 1],
+                    scale=SCALE,
+                    accum_out=unit[("rs", n)][:, j:j + 1],
+                )
+                chunk[("e", n, j)] = e_sb
+
+        def e_transposes(n, half):
+            et = ps_t.tile([P, 2, 256], F32, name="et", tag="tr")
+            for i in range(2):
+                e_sb = chunk[("e", n, 2 * half + i)]
+                for u in range(2):
+                    nc.tensor.transpose(et[:, u, i * P:(i + 1) * P], e_sb[:].bitcast(F32)[:, u * P:(u + 1) * P],
+                                        ident_f[:])
+            unit[("et", n, half)] = et
+
+        def regroup(n, half):
+            if half == 0:
+                unit[("g", n)] = gpool.tile([P, N, 4], BF16, name="grp", align_bytes=64)
+            nc.scalar.copy(
+                out=unit[("g", n)][:, 256 * half:256 * half + 256, :].bitcast(F32),
+                in_=unit[("et", n, half)][:].rearrange("p u q -> p q u"),
+            )
+
+        def quantise_e(n):
+            codes = gpool.tile([P, N], U32, name="codes", align_bytes=64)
+            scl = gpool.tile([P, N], U8, name="scl", align_bytes=64)
+            nc.vector.quantize_mx(
+                out=codes[:].bitcast(FP8X4),
+                scales=scl[:],
+                in_=unit[("g", n)][:].rearrange("p q t -> p (q t)"),
+            )
+            unit[("codes", n)] = codes
+            unit[("scl", n)] = scl
+
+        def mx_passes(n):
+            blk, vw = n // 2, n % 2
+            o_ps = ps_o.tile([P, 4, P], F32, name="o_ps")
+            for j in range(4):
+                nc.tensor.matmul_mx(
+                    out=o_ps[:, j, :],
+                    lhsT=unit[("codes", n)][:, j * P:(j + 1) * P].bitcast(FP8X4),
+                    lhsT_scale=unit[("scl", n)][:, j * P:(j + 1) * P],
+                    rhs=blk_t[("v_codes", blk)][:, vw * P:(vw + 1) * P].bitcast(FP8X4),
+                    rhs_scale=blk_t[("v_scl", blk)][:, vw * P:(vw + 1) * P],
+                    start=True,
+                    stop=True,
+                )
+            unit[("o_ps", n)] = o_ps
+
+        def normalise(n):
+            rinv = small.tile([P, 4], F32, name="rinv")
+            nc.vector.reciprocal(out=rinv[:], in_=unit[("rs", n)][:])
+            o_sb = opool.tile([P, 4, P], F32, name="o_sb")
+            nc.vector.tensor_tensor(
+                out=o_sb[:],
+                in0=unit[("o_ps", n)][:],
+                in1=rinv[:].unsqueeze(2).to_broadcast([P, 4, P]),
+                op=ALU.mult,
+            )
+            unit[("o_sb", n)] = o_sb
+
+        def o_transposes(n):
+            ot = ps_o.tile([P, N], F32, name="ot")
+            for j in range(4):
+                nc.tensor.transpose(ot[:, j * P:(j + 1) * P], unit[("o_sb", n)][:, j, :], ident_f[:])
+            unit[("ot", n)] = ot
+
+        def o_out(n):
+            blk, vw = n // 2, n % 2
+            if vw == 0:
+                blk_t[("out", blk)] = opool.tile([P, HPIX], F32, name="out_sb")
+            out_sb = blk_t[("out", blk)]
+            dst = out_sb[:].rearrange("c (h v x) -> c h v x", h=16, v=2)[:, :, vw, :]
+            src = unit[("ot", n)][:].rearrange("c (h x) -> c h x", h=16)
+            if OE_DVE_EVERY and n % OE_DVE_EVERY == 1:
+                nc.vector.tensor_copy(out=dst, in_=src)
+            else:
+                nc.scalar.copy(out=dst, in_=src)
+            if vw == 1:
+                nc.sync.dma_start(out=out_v[blk // NBD, blk % NBD], in_=out_sb[:])
+
+        def ok(n):
+            return 0 <= n < NUNITS
+
+        load_mask(0)
+        load_one("q_raw", 0)
+        load_one("k_raw", 0)
+        load_mask(1)
+        load_one("v_raw", 0)
+        load_blk(1)
+        load_blk(2)
+        load_mask(2)
+        load_mask(3)
+        for half in range(2):
+            mask_transposes(0, half)
+            mask_scale(0, half, half == 0)
+        to_windows("q", 0)
+
+        for m in range(NUNITS + 5):
+            blk, vw = m // 2, m % 2
+            nxt = blk + 1
+            late_mask = {4: 2, 6: 3}.get(m)
+            if vw == 0 and 1 <= blk and blk + 2 < NBLK:
+                load_blk(blk + 2)
+            if ok(m):
+                scores(m, 0, True)
+            if ok(m - 1):
+                e_transposes(m - 1, 0)
+                regroup(m - 1, 0)
+            if vw == 0 and 1 <= blk < NBLK:
+                v_regroup(blk, VE_ON_ACT)
+            if ok(m):
+                scores(m, 1, not ok(m - 3))
+            if ok(m - 3):
+                mx_passes(m - 3)
+            if ok(m):
+                scores(m, 2, True)
+                scores(m, 3, True)
+            if ok(m - 1):
+                e_transposes(m - 1, 1)
+            if ok(m - 4):
+                o_transposes(m - 4)
+            if m == 0:
+                mask_transposes(1, 0)
+            if vw == 1 and nxt < NBLK:
+                v_transposes(nxt)
+            if ok(m):
+                row_max(m, 0)
+            if ok(m - 2):
+                quantise_e(m - 2)
+            if ok(m - 3):
+                normalise(m - 3)
+            if ok(m):
+                row_max(m, 1)
+            if m == 0:
+                to_windows("v", 0)
+            if vw == 0 and nxt < NBLK:
+                to_windows("v", nxt)
+                to_windows("q", nxt)
+            if vw == 0 and 1 <= blk < NBLK:
+                quantise_v(blk)
+            if late_mask is not None:
+                mask_transposes(late_mask, 0)
+                mask_scale(late_mask, 0, False)
+            if ok(m):
+                exps(m, 0)
+            if m == 0:
+                mask_scale(1, 0, True)
+                mask_transposes(1, 1)
+            if ok(m - 1):
+                regroup(m - 1, 1)
+            if late_mask is not None:
+                mask_transposes(late_mask, 1)
+                mask_scale(late_mask, 1, False)
+            if ok(m - 4):
+                o_out(m - 4)
+            if ok(m):
+                exps(m, 1)
+            if m == 0:
+                mask_scale(1, 1, True)
+                v_transposes(0)
+                v_regroup(0, False)
+                quantise_v(0)

@@ -24,9 +24,11 @@ SCALE = 1.0 / SQRT_CH
 FLOPS = NUNITS * 2 * (2 * N * N * P)
 
 MANUAL = True
-NB_ON_POOL = False
+NB_ON_POOL = True
+DMA_WINDOWS = ('q', 'v')
 VE_ON_ACT = True
-OE_DVE_EVERY = 4
+DVE_MASK = (3,)
+OE_DVE_EVERY = 0
 
 
 def tile_window_attention_kernel(tc, kv, q, mask, out):
@@ -40,10 +42,11 @@ def tile_window_attention_kernel(tc, kv, q, mask, out):
         const = ctx.enter_context(tc.tile_pool(name="const", bufs=1))
         raw = ctx.enter_context(tc.tile_pool(name="raw", bufs=4))
         mraw = ctx.enter_context(tc.tile_pool(name="mraw", bufs=4))
-        win = ctx.enter_context(tc.tile_pool(name="win", bufs=3))
+        win = ctx.enter_context(tc.tile_pool(name="win", bufs=4))
         vq = ctx.enter_context(tc.tile_pool(name="vq", bufs=4))
-        small = ctx.enter_context(tc.tile_pool(name="small", bufs=8))
+        small = ctx.enter_context(tc.tile_pool(name="small", bufs=10))
         epool = ctx.enter_context(tc.tile_pool(name="epool", bufs=8))
+        spool = ctx.enter_context(tc.tile_pool(name="spool", bufs=3))
         gpool = ctx.enter_context(tc.tile_pool(name="gpool", bufs=4))
         opool = ctx.enter_context(tc.tile_pool(name="opool", bufs=3))
         ps_s = ctx.enter_context(tc.psum_pool(name="ps_s", bufs=4))
@@ -86,16 +89,27 @@ def tile_window_attention_kernel(tc, kv, q, mask, out):
 
         def load_one(what, blk):
             uw, bd = blk // NBD, blk % NBD
-            t = raw.tile([P, HPIX], BF16, name=what)
-            src = {"q_raw": q_v[uw, bd], "k_raw": kv_v[0, uw, bd], "v_raw": kv_v[1, uw, bd]}[what]
-            nc.sync.dma_start(out=t[:], in_=src)
-            blk_t[(what, blk)] = t
+            src = {"q": q_v[uw, bd], "k": kv_v[0, uw, bd], "v": kv_v[1, uw, bd]}[what]
+            if what in DMA_WINDOWS:
+                t = win.tile([P, 2, N], BF16, name=what + "_win")
+                for vw in range(2):
+                    nc.sync.dma_start(
+                        out=t[:, vw, :].rearrange("c (h w) -> c h w", h=16),
+                        in_=src.rearrange("c (h v w) -> c h v w", h=16, v=2)[:, :, vw, :],
+                    )
+                blk_t[(what + "_win", blk)] = t
+            else:
+                t = raw.tile([P, HPIX], BF16, name=what + "_raw")
+                nc.sync.dma_start(out=t[:], in_=src)
+                blk_t[(what + "_raw", blk)] = t
 
         def load_blk(blk):
-            for what in ("q_raw", "k_raw", "v_raw"):
+            for what in ("q", "k", "v"):
                 load_one(what, blk)
 
         def to_windows(what, blk):
+            if what in DMA_WINDOWS:
+                return
             dst = win.tile([P, 2, N], BF16, name=what + "_win")
             nc.vector.tensor_copy(
                 out=dst[:].rearrange("c v (h w) -> c v h w", h=16),
@@ -137,6 +151,10 @@ def tile_window_attention_kernel(tc, kv, q, mask, out):
             lhs = blk_t[("q_win", blk)][:, vw, j * P:(j + 1) * P]
             rhs = blk_t[("k_raw", blk)][:].rearrange("c (h v x) -> c h v x", h=16, v=2)[:, :, vw, :]
             s_ps = ps_s.tile([P, N], F32, name="s_ps")
+            chunk[("s", n, j)] = s_ps
+            if j in DVE_MASK:
+                nc.tensor.matmul(out=s_ps[:], lhsT=lhs, rhs=rhs, start=True, stop=True)
+                return
             if mm_first:
                 nc.tensor.matmul(out=s_ps[:], lhsT=lhs, rhs=rhs, start=True, stop=False)
             for t in range(4):
@@ -150,19 +168,33 @@ def tile_window_attention_kernel(tc, kv, q, mask, out):
                 )
             if not mm_first:
                 nc.tensor.matmul(out=s_ps[:], lhsT=lhs, rhs=rhs, start=False, stop=True)
-            chunk[("s", n, j)] = s_ps
 
         def row_max(n, half):
+            w = 2 * (n // 2 // NBD) + n % 2
             nm = small.tile([P, 2], F32, name="nm")
-            for i in range(2):
-                nc.vector.tensor_reduce(out=nm[:, i:i + 1], in_=chunk[("s", n, 2 * half + i)][:], axis=AX.X,
-                                        op=ALU.max, negate=True)
             nb = small.tile([P, 2], F32, name="nb")
-            if NB_ON_POOL:
-                nc.gpsimd.tensor_scalar(out=nb[:], in0=nm[:], scalar1=SCALE, scalar2=0.0, op0=ALU.mult, op1=ALU.add)
-            else:
-                nc.vector.tensor_scalar_mul(out=nb[:], in0=nm[:], scalar1=SCALE)
-            chunk[("nb", n, half)] = nb
+            for i in range(2):
+                j = 2 * half + i
+                src = chunk[("s", n, j)]
+                if j in DVE_MASK:
+                    s_sb = spool.tile([P, N], F32, name="s_sb")
+                    nc.vector.scalar_tensor_tensor(out=s_sb[:], in0=src[:], scalar=SCALE, in1=blk_t[("m", w)][:, j, :],
+                                                   op0=ALU.mult, op1=ALU.add)
+                    chunk[("s", n, j)] = s_sb
+                    nd = small.tile([P, 1], F32, name="nd")
+                    nc.vector.tensor_reduce(out=nd[:], in_=s_sb[:], axis=AX.X, op=ALU.max, negate=True)
+                    chunk[("nb", n, j)] = nd[:]
+                else:
+                    nc.vector.tensor_reduce(out=nm[:, i:i + 1], in_=src[:], axis=AX.X, op=ALU.max, negate=True)
+                    chunk[("nb", n, j)] = nb[:, i:i + 1]
+            cols = [i for i in range(2) if 2 * half + i not in DVE_MASK]
+            if cols:
+                lo, hi = cols[0], cols[-1] + 1
+                if NB_ON_POOL:
+                    nc.gpsimd.tensor_scalar(out=nb[:, lo:hi], in0=nm[:, lo:hi], scalar1=SCALE, scalar2=0.0,
+                                            op0=ALU.mult, op1=ALU.add)
+                else:
+                    nc.vector.tensor_scalar_mul(out=nb[:, lo:hi], in0=nm[:, lo:hi], scalar1=SCALE)
 
         def exps(n, half):
             if half == 0:
@@ -174,8 +206,8 @@ def tile_window_attention_kernel(tc, kv, q, mask, out):
                     out=e_sb[:],
                     in_=chunk[("s", n, j)][:],
                     func=AF.Exp,
-                    bias=chunk[("nb", n, half)][:, i:i + 1],
-                    scale=SCALE,
+                    bias=chunk[("nb", n, j)],
+                    scale=(1.0 if j in DVE_MASK else SCALE),
                     accum_out=unit[("rs", n)][:, j:j + 1],
                 )
                 chunk[("e", n, j)] = e_sb
@@ -259,10 +291,10 @@ def tile_window_attention_kernel(tc, kv, q, mask, out):
             return 0 <= n < NUNITS
 
         load_mask(0)
-        load_one("q_raw", 0)
-        load_one("k_raw", 0)
+        load_one("q", 0)
+        load_one("k", 0)
         load_mask(1)
-        load_one("v_raw", 0)
+        load_one("v", 0)
         load_blk(1)
         load_blk(2)
         load_mask(2)

@@ -24,7 +24,7 @@ SCALE = 1.0 / SQRT_CH
 FLOPS = NUNITS * 2 * (2 * N * N * P)
 
 MANUAL = True
-NB_ON_POOL = True
+FUSED_MAX = True
 DMA_WINDOWS = ('q', 'v')
 VE_ON_ACT = True
 DVE_MASK = (3,)
@@ -44,7 +44,7 @@ def tile_window_attention_kernel(tc, kv, q, mask, out):
         mraw = ctx.enter_context(tc.tile_pool(name="mraw", bufs=4))
         win = ctx.enter_context(tc.tile_pool(name="win", bufs=4))
         vq = ctx.enter_context(tc.tile_pool(name="vq", bufs=4))
-        small = ctx.enter_context(tc.tile_pool(name="small", bufs=10))
+        small = ctx.enter_context(tc.tile_pool(name="small", bufs=12))
         epool = ctx.enter_context(tc.tile_pool(name="epool", bufs=8))
         spool = ctx.enter_context(tc.tile_pool(name="spool", bufs=3))
         gpool = ctx.enter_context(tc.tile_pool(name="gpool", bufs=4))
@@ -169,32 +169,25 @@ def tile_window_attention_kernel(tc, kv, q, mask, out):
             if not mm_first:
                 nc.tensor.matmul(out=s_ps[:], lhsT=lhs, rhs=rhs, start=False, stop=True)
 
-        def row_max(n, half):
+        def row_max(n, j):
             w = 2 * (n // 2 // NBD) + n % 2
-            nm = small.tile([P, 2], F32, name="nm")
-            nb = small.tile([P, 2], F32, name="nb")
-            for i in range(2):
-                j = 2 * half + i
-                src = chunk[("s", n, j)]
-                if j in DVE_MASK:
-                    s_sb = spool.tile([P, N], F32, name="s_sb")
-                    nc.vector.scalar_tensor_tensor(out=s_sb[:], in0=src[:], scalar=SCALE, in1=blk_t[("m", w)][:, j, :],
-                                                   op0=ALU.mult, op1=ALU.add)
-                    chunk[("s", n, j)] = s_sb
-                    nd = small.tile([P, 1], F32, name="nd")
-                    nc.vector.tensor_reduce(out=nd[:], in_=s_sb[:], axis=AX.X, op=ALU.max, negate=True)
-                    chunk[("nb", n, j)] = nd[:]
-                else:
-                    nc.vector.tensor_reduce(out=nm[:, i:i + 1], in_=src[:], axis=AX.X, op=ALU.max, negate=True)
-                    chunk[("nb", n, j)] = nb[:, i:i + 1]
-            cols = [i for i in range(2) if 2 * half + i not in DVE_MASK]
-            if cols:
-                lo, hi = cols[0], cols[-1] + 1
-                if NB_ON_POOL:
-                    nc.gpsimd.tensor_scalar(out=nb[:, lo:hi], in0=nm[:, lo:hi], scalar1=SCALE, scalar2=0.0,
-                                            op0=ALU.mult, op1=ALU.add)
-                else:
-                    nc.vector.tensor_scalar_mul(out=nb[:, lo:hi], in0=nm[:, lo:hi], scalar1=SCALE)
+            src = chunk[("s", n, j)]
+            nb = small.tile([P, 1], F32, name="nb")
+            if j in DVE_MASK:
+                s_sb = spool.tile([P, N], F32, name="s_sb")
+                nc.vector.scalar_tensor_tensor(out=s_sb[:], in0=src[:], scalar=SCALE, in1=blk_t[("m", w)][:, j, :],
+                                               op0=ALU.mult, op1=ALU.add)
+                chunk[("s", n, j)] = s_sb
+                nc.vector.tensor_reduce(out=nb[:], in_=s_sb[:], axis=AX.X, op=ALU.max, negate=True)
+            elif FUSED_MAX:
+                junk = spool.tile([P, N], BF16, name="junk")
+                nc.vector.tensor_scalar(out=junk[:], in0=src[:], scalar1=-SCALE, scalar2=None, op0=ALU.mult,
+                                        op1=ALU.min, accum_out=nb[:])
+            else:
+                nm = small.tile([P, 1], F32, name="nm")
+                nc.vector.tensor_reduce(out=nm[:], in_=src[:], axis=AX.X, op=ALU.max, negate=True)
+                nc.vector.tensor_scalar_mul(out=nb[:], in0=nm[:], scalar1=SCALE)
+            chunk[("nb", n, j)] = nb[:]
 
         def exps(n, half):
             if half == 0:
@@ -290,6 +283,10 @@ def tile_window_attention_kernel(tc, kv, q, mask, out):
         def ok(n):
             return 0 <= n < NUNITS
 
+        warm = const.tile([P, 1], F32, name="warm")
+        nc.vector.memset(warm[:], 0.0)
+        nc.scalar.activation(out=warm[:], in_=warm[:], func=AF.Exp)
+
         load_mask(0)
         load_one("q", 0)
         load_one("k", 0)
@@ -334,12 +331,15 @@ def tile_window_attention_kernel(tc, kv, q, mask, out):
                 v_transposes(nxt)
             if ok(m):
                 row_max(m, 0)
+                row_max(m, 1)
             if ok(m - 2):
                 quantise_e(m - 2)
+            if ok(m):
+                row_max(m, 2)
             if ok(m - 3):
                 normalise(m - 3)
             if ok(m):
-                row_max(m, 1)
+                row_max(m, 3)
             if m == 0:
                 to_windows("v", 0)
             if vw == 0 and nxt < NBLK:

@@ -27,8 +27,8 @@ MANUAL = True
 FUSED_MAX = True
 DMA_WINDOWS = ('q', 'v')
 VE_ON_ACT = True
-DVE_MASK = (3,)
-OE_DVE_EVERY = 0
+DVE_MASK = ()
+OE_ON_ACT = ()
 
 
 def tile_window_attention_kernel(tc, kv, q, mask, out):
@@ -273,10 +273,10 @@ def tile_window_attention_kernel(tc, kv, q, mask, out):
             out_sb = blk_t[("out", blk)]
             dst = out_sb[:].rearrange("c (h v x) -> c h v x", h=16, v=2)[:, :, vw, :]
             src = unit[("ot", n)][:].rearrange("c (h x) -> c h x", h=16)
-            if OE_DVE_EVERY and n % OE_DVE_EVERY == 1:
-                nc.vector.tensor_copy(out=dst, in_=src)
-            else:
+            if n % 4 in OE_ON_ACT:
                 nc.scalar.copy(out=dst, in_=src)
+            else:
+                nc.vector.tensor_copy(out=dst, in_=src)
             if vw == 1:
                 nc.sync.dma_start(out=out_v[blk // NBD, blk % NBD], in_=out_sb[:])
 

@@ -24,11 +24,12 @@ SCALE = 1.0 / SQRT_CH
 FLOPS = NUNITS * 2 * (2 * N * N * P)
 
 MANUAL = True
+S_SB_BUFS = 8
 FUSED_MAX = True
 DMA_WINDOWS = ('q', 'v')
 VE_ON_ACT = True
 DVE_MASK = ()
-OE_ON_ACT = ()
+OE_ON_ACT = (0,)
 
 
 def tile_window_attention_kernel(tc, kv, q, mask, out):
@@ -44,9 +45,9 @@ def tile_window_attention_kernel(tc, kv, q, mask, out):
         mraw = ctx.enter_context(tc.tile_pool(name="mraw", bufs=4))
         win = ctx.enter_context(tc.tile_pool(name="win", bufs=4))
         vq = ctx.enter_context(tc.tile_pool(name="vq", bufs=4))
-        small = ctx.enter_context(tc.tile_pool(name="small", bufs=12))
+        small = ctx.enter_context(tc.tile_pool(name="small", bufs=16))
         epool = ctx.enter_context(tc.tile_pool(name="epool", bufs=8))
-        spool = ctx.enter_context(tc.tile_pool(name="spool", bufs=3))
+        spool = ctx.enter_context(tc.tile_pool(name="spool", bufs=S_SB_BUFS))
         gpool = ctx.enter_context(tc.tile_pool(name="gpool", bufs=4))
         opool = ctx.enter_context(tc.tile_pool(name="opool", bufs=3))
         ps_s = ctx.enter_context(tc.psum_pool(name="ps_s", bufs=4))
@@ -145,29 +146,29 @@ def tile_window_attention_kernel(tc, kv, q, mask, out):
             blk_t[("v_codes", blk)] = v_codes
             blk_t[("v_scl", blk)] = v_scl
 
-        def scores(n, j, mm_first):
-            blk, vw = n // 2, n % 2
-            w = 2 * (blk // NBD) + vw
-            lhs = blk_t[("q_win", blk)][:, vw, j * P:(j + 1) * P]
-            rhs = blk_t[("k_raw", blk)][:].rearrange("c (h v x) -> c h v x", h=16, v=2)[:, :, vw, :]
+        def add_mask(n, j):
+            w = 2 * (n // 2 // NBD) + n % 2
             s_ps = ps_s.tile([P, N], F32, name="s_ps")
             chunk[("s", n, j)] = s_ps
-            if j in DVE_MASK:
-                nc.tensor.matmul(out=s_ps[:], lhsT=lhs, rhs=rhs, start=True, stop=True)
-                return
-            if mm_first:
-                nc.tensor.matmul(out=s_ps[:], lhsT=lhs, rhs=rhs, start=True, stop=False)
             for t in range(4):
                 nc.tensor.matmul(
                     out=s_ps[:, t * P:(t + 1) * P],
                     lhsT=mask_t[:, w, t, j * P:(j + 1) * P],
                     rhs=ident_f[:],
                     is_transpose=True,
-                    start=(t == 0 and not mm_first),
-                    stop=(t == 3 and mm_first),
+                    start=(t == 0),
+                    stop=False,
                 )
-            if not mm_first:
-                nc.tensor.matmul(out=s_ps[:], lhsT=lhs, rhs=rhs, start=False, stop=True)
+
+        def add_qk(n, j):
+            blk, vw = n // 2, n % 2
+            nc.tensor.matmul(
+                out=chunk[("s", n, j)][:],
+                lhsT=blk_t[("q_win", blk)][:, vw, j * P:(j + 1) * P],
+                rhs=blk_t[("k_raw", blk)][:].rearrange("c (h v x) -> c h v x", h=16, v=2)[:, :, vw, :],
+                start=False,
+                stop=True,
+            )
 
         def row_max(n, j):
             w = 2 * (n // 2 // NBD) + n % 2
@@ -180,9 +181,10 @@ def tile_window_attention_kernel(tc, kv, q, mask, out):
                 chunk[("s", n, j)] = s_sb
                 nc.vector.tensor_reduce(out=nb[:], in_=s_sb[:], axis=AX.X, op=ALU.max, negate=True)
             elif FUSED_MAX:
-                junk = spool.tile([P, N], BF16, name="junk")
-                nc.vector.tensor_scalar(out=junk[:], in0=src[:], scalar1=-SCALE, scalar2=None, op0=ALU.mult,
+                s_neg = spool.tile([P, N], F32, name="s_neg")
+                nc.vector.tensor_scalar(out=s_neg[:], in0=src[:], scalar1=-SCALE, scalar2=None, op0=ALU.mult,
                                         op1=ALU.min, accum_out=nb[:])
+                chunk[("s", n, j)] = s_neg
             else:
                 nm = small.tile([P, 1], F32, name="nm")
                 nc.vector.tensor_reduce(out=nm[:], in_=src[:], axis=AX.X, op=ALU.max, negate=True)
@@ -200,7 +202,7 @@ def tile_window_attention_kernel(tc, kv, q, mask, out):
                     in_=chunk[("s", n, j)][:],
                     func=AF.Exp,
                     bias=chunk[("nb", n, j)],
-                    scale=(1.0 if j in DVE_MASK else SCALE),
+                    scale=(1.0 if j in DVE_MASK else -1.0),
                     accum_out=unit[("rs", n)][:, j:j + 1],
                 )
                 chunk[("e", n, j)] = e_sb
@@ -308,19 +310,23 @@ def tile_window_attention_kernel(tc, kv, q, mask, out):
             if vw == 0 and 1 <= blk and blk + 2 < NBLK:
                 load_blk(blk + 2)
             if ok(m):
-                scores(m, 0, True)
+                add_mask(m, 0)
+                add_qk(m, 0)
             if ok(m - 1):
                 e_transposes(m - 1, 0)
                 regroup(m - 1, 0)
             if vw == 0 and 1 <= blk < NBLK:
                 v_regroup(blk, VE_ON_ACT)
             if ok(m):
-                scores(m, 1, not ok(m - 3))
+                add_mask(m, 1)
+                add_qk(m, 1)
+                add_mask(m, 2)
+                add_mask(m, 3)
+                add_qk(m, 2)
             if ok(m - 3):
                 mx_passes(m - 3)
             if ok(m):
-                scores(m, 2, True)
-                scores(m, 3, True)
+                add_qk(m, 3)
             if ok(m - 1):
                 e_transposes(m - 1, 1)
             if ok(m - 4):

@@ -24,12 +24,13 @@ SCALE = 1.0 / SQRT_CH
 FLOPS = NUNITS * 2 * (2 * N * N * P)
 
 MANUAL = True
+ALL = (0, 1, 2, 3)
 S_SB_BUFS = 8
 FUSED_MAX = True
 DMA_WINDOWS = ('q', 'v')
 VE_ON_ACT = True
 DVE_MASK = ()
-OE_ON_ACT = (0,)
+OE_ON_ACT = ()
 
 
 def tile_window_attention_kernel(tc, kv, q, mask, out):
@@ -88,17 +89,17 @@ def tile_window_attention_kernel(tc, kv, q, mask, out):
             else:
                 nc.vector.tensor_scalar_mul(out=dst, in0=src, scalar1=SQRT_CH)
 
-        def load_one(what, blk):
+        def load_one(what, blk, vws=(0, 1)):
             uw, bd = blk // NBD, blk % NBD
             src = {"q": q_v[uw, bd], "k": kv_v[0, uw, bd], "v": kv_v[1, uw, bd]}[what]
             if what in DMA_WINDOWS:
-                t = win.tile([P, 2, N], BF16, name=what + "_win")
-                for vw in range(2):
+                if 0 in vws:
+                    blk_t[(what + "_win", blk)] = win.tile([P, 2, N], BF16, name=what + "_win")
+                for vw in vws:
                     nc.sync.dma_start(
-                        out=t[:, vw, :].rearrange("c (h w) -> c h w", h=16),
+                        out=blk_t[(what + "_win", blk)][:, vw, :].rearrange("c (h w) -> c h w", h=16),
                         in_=src.rearrange("c (h v w) -> c h v w", h=16, v=2)[:, :, vw, :],
                     )
-                blk_t[(what + "_win", blk)] = t
             else:
                 t = raw.tile([P, HPIX], BF16, name=what + "_raw")
                 nc.sync.dma_start(out=t[:], in_=src)
@@ -192,8 +193,8 @@ def tile_window_attention_kernel(tc, kv, q, mask, out):
             chunk[("nb", n, j)] = nb[:]
 
         def exps(n, half):
-            if half == 0:
-                unit[("rs", n)] = small.tile([P, 4], F32, name="rs")
+            if half == 0 and n % 2 == 0:
+                blk_t[("rs", n // 2)] = small.tile([P, 8], F32, name="rs")
             for i in range(2):
                 j = 2 * half + i
                 e_sb = epool.tile([P, N], BF16, name="e_sb")
@@ -203,7 +204,7 @@ def tile_window_attention_kernel(tc, kv, q, mask, out):
                     func=AF.Exp,
                     bias=chunk[("nb", n, j)],
                     scale=(1.0 if j in DVE_MASK else -1.0),
-                    accum_out=unit[("rs", n)][:, j:j + 1],
+                    accum_out=blk_t[("rs", n // 2)][:, 4 * (n % 2) + j:4 * (n % 2) + j + 1],
                 )
                 chunk[("e", n, j)] = e_sb
 
@@ -224,21 +225,24 @@ def tile_window_attention_kernel(tc, kv, q, mask, out):
                 in_=unit[("et", n, half)][:].rearrange("p u q -> p q u"),
             )
 
-        def quantise_e(n):
-            codes = gpool.tile([P, N], U32, name="codes", align_bytes=64)
-            scl = gpool.tile([P, N], U8, name="scl", align_bytes=64)
+        def quantise_e(n, js):
+            if js[0] == 0:
+                unit[("codes", n)] = gpool.tile([P, N], U32, name="codes", align_bytes=64)
+                unit[("scl", n)] = gpool.tile([P, N], U8, name="scl", align_bytes=64)
+            lo, hi = js[0] * P, (js[-1] + 1) * P
             nc.vector.quantize_mx(
-                out=codes[:].bitcast(FP8X4),
-                scales=scl[:],
-                in_=unit[("g", n)][:].rearrange("p q t -> p (q t)"),
+                out=unit[("codes", n)][:, lo:hi].bitcast(FP8X4),
+                scales=unit[("scl", n)][:, lo:hi],
+                in_=unit[("g", n)][:, lo:hi, :].rearrange("p q t -> p (q t)"),
             )
-            unit[("codes", n)] = codes
-            unit[("scl", n)] = scl
 
-        def mx_passes(n):
+        def mx_passes(n, js, spare=False):
             blk, vw = n // 2, n % 2
-            o_ps = ps_o.tile([P, 4, P], F32, name="o_ps")
-            for j in range(4):
+            if spare:
+                o_ps = ps_s.tile([P, 4, P], F32, name="o_ps", tag="s_ps")
+            else:
+                o_ps = ps_o.tile([P, 4, P], F32, name="o_ps")
+            for j in js:
                 nc.tensor.matmul_mx(
                     out=o_ps[:, j, :],
                     lhsT=unit[("codes", n)][:, j * P:(j + 1) * P].bitcast(FP8X4),
@@ -248,38 +252,46 @@ def tile_window_attention_kernel(tc, kv, q, mask, out):
                     start=True,
                     stop=True,
                 )
-            unit[("o_ps", n)] = o_ps
+            unit[("o_ps", n, js[0])] = o_ps
 
-        def normalise(n):
-            rinv = small.tile([P, 4], F32, name="rinv")
-            nc.vector.reciprocal(out=rinv[:], in_=unit[("rs", n)][:])
+        def normalise(n, js):
+            blk, vw = n // 2, n % 2
+            if vw == 0:
+                rinv = small.tile([P, 8], F32, name="rinv")
+                nc.vector.reciprocal(out=rinv[:], in_=blk_t[("rs", blk)][:])
+                blk_t[("rinv", blk)] = rinv
+            lo, hi = js[0], js[-1] + 1
             o_sb = opool.tile([P, 4, P], F32, name="o_sb")
             nc.vector.tensor_tensor(
-                out=o_sb[:],
-                in0=unit[("o_ps", n)][:],
-                in1=rinv[:].unsqueeze(2).to_broadcast([P, 4, P]),
+                out=o_sb[:, lo:hi, :],
+                in0=unit[("o_ps", n, lo)][:, lo:hi, :],
+                in1=blk_t[("rinv", blk)][:, 4 * vw + lo:4 * vw + hi].unsqueeze(2).to_broadcast([P, hi - lo, P]),
                 op=ALU.mult,
             )
-            unit[("o_sb", n)] = o_sb
+            unit[("o_sb", n, lo)] = o_sb
 
-        def o_transposes(n):
-            ot = ps_o.tile([P, N], F32, name="ot")
-            for j in range(4):
-                nc.tensor.transpose(ot[:, j * P:(j + 1) * P], unit[("o_sb", n)][:, j, :], ident_f[:])
-            unit[("ot", n)] = ot
+        def o_transposes(n, js, spare=False):
+            if spare:
+                ot = ps_s.tile([P, N], F32, name="ot", tag="s_ps")
+            else:
+                ot = ps_o.tile([P, N], F32, name="ot")
+            for j in js:
+                nc.tensor.transpose(ot[:, j * P:(j + 1) * P], unit[("o_sb", n, js[0])][:, j, :], ident_f[:])
+            unit[("ot", n, js[0])] = ot
 
-        def o_out(n):
+        def o_out(n, js, on_scalar):
             blk, vw = n // 2, n % 2
             if vw == 0:
                 blk_t[("out", blk)] = opool.tile([P, HPIX], F32, name="out_sb")
             out_sb = blk_t[("out", blk)]
-            dst = out_sb[:].rearrange("c (h v x) -> c h v x", h=16, v=2)[:, :, vw, :]
-            src = unit[("ot", n)][:].rearrange("c (h x) -> c h x", h=16)
-            if n % 4 in OE_ON_ACT:
+            h0, h1 = 4 * js[0], 4 * (js[-1] + 1)
+            dst = out_sb[:].rearrange("c (h v x) -> c h v x", h=16, v=2)[:, h0:h1, vw, :]
+            src = unit[("ot", n, js[0])][:, js[0] * P:(js[-1] + 1) * P].rearrange("c (h x) -> c h x", x=32)
+            if on_scalar:
                 nc.scalar.copy(out=dst, in_=src)
             else:
                 nc.vector.tensor_copy(out=dst, in_=src)
-            if vw == 1:
+            if vw == 1 and js[-1] == 3:
                 nc.sync.dma_start(out=out_v[blk // NBD, blk % NBD], in_=out_sb[:])
 
         def ok(n):
@@ -290,8 +302,9 @@ def tile_window_attention_kernel(tc, kv, q, mask, out):
         nc.scalar.activation(out=warm[:], in_=warm[:], func=AF.Exp)
 
         load_mask(0)
-        load_one("q", 0)
+        load_one("q", 0, (0,))
         load_one("k", 0)
+        load_one("q", 0, (1,))
         load_mask(1)
         load_one("v", 0)
         load_blk(1)
@@ -303,7 +316,7 @@ def tile_window_attention_kernel(tc, kv, q, mask, out):
             mask_scale(0, half, half == 0)
         to_windows("q", 0)
 
-        for m in range(NUNITS + 5):
+        for m in range(NUNITS):
             blk, vw = m // 2, m % 2
             nxt = blk + 1
             late_mask = {4: 2, 6: 3}.get(m)
@@ -324,13 +337,13 @@ def tile_window_attention_kernel(tc, kv, q, mask, out):
                 add_mask(m, 3)
                 add_qk(m, 2)
             if ok(m - 3):
-                mx_passes(m - 3)
+                mx_passes(m - 3, ALL)
             if ok(m):
                 add_qk(m, 3)
             if ok(m - 1):
                 e_transposes(m - 1, 1)
             if ok(m - 4):
-                o_transposes(m - 4)
+                o_transposes(m - 4, ALL)
             if m == 0:
                 mask_transposes(1, 0)
             if vw == 1 and nxt < NBLK:
@@ -339,11 +352,11 @@ def tile_window_attention_kernel(tc, kv, q, mask, out):
                 row_max(m, 0)
                 row_max(m, 1)
             if ok(m - 2):
-                quantise_e(m - 2)
+                quantise_e(m - 2, ALL)
             if ok(m):
                 row_max(m, 2)
             if ok(m - 3):
-                normalise(m - 3)
+                normalise(m - 3, ALL)
             if ok(m):
                 row_max(m, 3)
             if m == 0:
@@ -365,13 +378,37 @@ def tile_window_attention_kernel(tc, kv, q, mask, out):
                 regroup(m - 1, 1)
             if late_mask is not None:
                 mask_transposes(late_mask, 1)
-                mask_scale(late_mask, 1, False)
+                mask_scale(late_mask, 1, True)
             if ok(m - 4):
-                o_out(m - 4)
+                o_out(m - 4, ALL, (m - 4) % 4 in OE_ON_ACT)
             if ok(m):
                 exps(m, 1)
             if m == 0:
-                mask_scale(1, 1, True)
+                mask_scale(1, 1, False)
                 v_transposes(0)
                 v_regroup(0, False)
                 quantise_v(0)
+
+        z = NUNITS - 1
+        first, second = (0, 1), (2, 3)
+        e_transposes(z, 0)
+        regroup(z, 0)
+        mx_passes(z - 2, ALL)
+        e_transposes(z, 1)
+        o_transposes(z - 3, ALL)
+        quantise_e(z - 1, ALL)
+        normalise(z - 2, ALL)
+        quantise_e(z, first)
+        regroup(z, 1)
+        quantise_e(z, second)
+        o_out(z - 3, ALL, True)
+        mx_passes(z - 1, ALL, True)
+        mx_passes(z, first, True)
+        o_transposes(z - 2, ALL)
+        o_out(z - 2, ALL, True)
+        mx_passes(z, second, True)
+        for n, js in ((z - 1, ALL), (z, first), (z, second)):
+            normalise(n, js)
+        for n, js in ((z - 1, ALL), (z, first), (z, second)):
+            o_transposes(n, js, True)
+            o_out(n, js, True)

@@ -23,7 +23,7 @@ SQRT_CH = math.sqrt(128.0)
 SCALE = 1.0 / SQRT_CH
 FLOPS = NUNITS * 2 * (2 * N * N * P)
 
-MANUAL = True
+MANUAL = False
 ALL = (0, 1, 2, 3)
 S_SB_BUFS = 8
 FUSED_MAX = True

import math
from contextlib import ExitStack

import concourse.mybir as mybir
from concourse.masks import make_identity

F32 = mybir.dt.float32
BF16 = mybir.dt.bfloat16
U32 = mybir.dt.uint32
U8 = mybir.dt.uint8
FP8X4 = mybir.dt.float8_e4m3fn_x4
AF = mybir.ActivationFunctionType
ALU = mybir.AluOpType
AX = mybir.AxisListType

P = 128
NB, HEADS, NWIN, N = 2, 6, 4, 512
NBD = NB * HEADS
NBLK = 2 * NBD
NUNITS = 2 * NBLK
HPIX = 1024
SQRT_CH = math.sqrt(128.0)
SCALE = 1.0 / SQRT_CH
FLOPS = NUNITS * 2 * (2 * N * N * P)

MANUAL = False
ALL = (0, 1, 2, 3)
S_SB_BUFS = 8
FUSED_MAX = True
DMA_WINDOWS = ('q', 'v')
VE_ON_ACT = True
DVE_MASK = ()
OE_ON_ACT = ()


def tile_window_attention_kernel(tc, kv, q, mask, out):
    nc = tc.nc
    q_v = q.rearrange("b (d c) (u h) w -> u (b d) c (h w)", c=P, u=2)
    kv_v = kv.rearrange("s b (d c) (u h) w -> s u (b d) c (h w)", c=P, u=2)
    out_v = out.rearrange("b (d c) (u h) w -> u (b d) c (h w)", c=P, u=2)
    mask_v = mask.rearrange("w (j p) k -> w p j k", p=P)

    with ExitStack() as ctx:
        const = ctx.enter_context(tc.tile_pool(name="const", bufs=1))
        raw = ctx.enter_context(tc.tile_pool(name="raw", bufs=4))
        mraw = ctx.enter_context(tc.tile_pool(name="mraw", bufs=4))
        win = ctx.enter_context(tc.tile_pool(name="win", bufs=4))
        vq = ctx.enter_context(tc.tile_pool(name="vq", bufs=4))
        small = ctx.enter_context(tc.tile_pool(name="small", bufs=16))
        epool = ctx.enter_context(tc.tile_pool(name="epool", bufs=8))
        spool = ctx.enter_context(tc.tile_pool(name="spool", bufs=S_SB_BUFS))
        gpool = ctx.enter_context(tc.tile_pool(name="gpool", bufs=4))
        opool = ctx.enter_context(tc.tile_pool(name="opool", bufs=3))
        ps_s = ctx.enter_context(tc.psum_pool(name="ps_s", bufs=4))
        ps_t = ctx.enter_context(tc.psum_pool(name="ps_t", bufs=2))
        ps_o = ctx.enter_context(tc.psum_pool(name="ps_o", bufs=1))
        if MANUAL:
            ctx.enter_context(tc.manual_schedule())

        ident_b = const.tile([P, P], BF16, name="ident_b")
        ident_f = const.tile([P, P], F32, name="ident_f")
        make_identity(nc, ident_b[:])
        make_identity(nc, ident_f[:])
        mask_t = const.tile([P, NWIN, 4, N], F32, name="mask_t")

        blk_t = {}
        unit = {}
        chunk = {}

        def load_mask(w):
            m_sb = mraw.tile([P, 4, N], BF16, name="m_sb")
            nc.sync.dma_start(out=m_sb[:], in_=mask_v[w])
            blk_t[("m", w)] = m_sb

        def mask_transposes(w, half):
            m_sb = blk_t[("m", w)]
            mt = ps_t.tile([P, 2, N], BF16, name="mt", tag="tr")
            for ti in range(2):
                for j in range(4):
                    t = 2 * half + ti
                    nc.tensor.transpose(mt[:, ti, j * P:(j + 1) * P], m_sb[:, j, t * P:(t + 1) * P], ident_b[:])
            blk_t[("mt", w, half)] = mt

        def mask_scale(w, half, on_scalar):
            dst = mask_t[:, w, 2 * half:2 * half + 2, :]
            src = blk_t[("mt", w, half)][:]
            if on_scalar:
                nc.scalar.mul(out=dst, in_=src, mul=SQRT_CH)
            else:
                nc.vector.tensor_scalar_mul(out=dst, in0=src, scalar1=SQRT_CH)

        def load_one(what, blk, vws=(0, 1)):
            uw, bd = blk // NBD, blk % NBD
            src = {"q": q_v[uw, bd], "k": kv_v[0, uw, bd], "v": kv_v[1, uw, bd]}[what]
            if what in DMA_WINDOWS:
                if 0 in vws:
                    blk_t[(what + "_win", blk)] = win.tile([P, 2, N], BF16, name=what + "_win")
                for vw in vws:
                    nc.sync.dma_start(
                        out=blk_t[(what + "_win", blk)][:, vw, :].rearrange("c (h w) -> c h w", h=16),
                        in_=src.rearrange("c (h v w) -> c h v w", h=16, v=2)[:, :, vw, :],
                    )
            else:
                t = raw.tile([P, HPIX], BF16, name=what + "_raw")
                nc.sync.dma_start(out=t[:], in_=src)
                blk_t[(what + "_raw", blk)] = t

        def load_blk(blk):
            for what in ("q", "k", "v"):
                load_one(what, blk)

        def to_windows(what, blk):
            if what in DMA_WINDOWS:
                return
            dst = win.tile([P, 2, N], BF16, name=what + "_win")
            nc.vector.tensor_copy(
                out=dst[:].rearrange("c v (h w) -> c v h w", h=16),
                in_=blk_t[(what + "_raw", blk)][:].rearrange("c (h v w) -> c v h w", h=16, v=2),
            )
            blk_t[(what + "_win", blk)] = dst

        def v_transposes(blk):
            v_win = blk_t[("v_win", blk)]
            vt = ps_t.tile([P, 2, 2, P], F32, name="vt", tag="tr")
            for vw in range(2):
                for u in range(2):
                    nc.tensor.transpose(vt[:, vw, u, :], v_win[:, vw, :].bitcast(F32)[:, u * P:(u + 1) * P], ident_f[:])
            blk_t[("vt", blk)] = vt

        def v_regroup(blk, on_scalar):
            vg = vq.tile([P, 2, P, 4], BF16, name="vg", align_bytes=64)
            src = blk_t[("vt", blk)][:].rearrange("p w u c -> p w c u")
            if on_scalar:
                nc.scalar.copy(out=vg[:].bitcast(F32), in_=src)
            else:
                nc.vector.tensor_copy(out=vg[:].bitcast(F32), in_=src)
            blk_t[("vg", blk)] = vg

        def quantise_v(blk):
            v_codes = vq.tile([P, 2 * P], U32, name="v_codes", align_bytes=64)
            v_scl = vq.tile([P, 2 * P], U8, name="v_scl", align_bytes=64)
            nc.vector.quantize_mx(
                out=v_codes[:].bitcast(FP8X4),
                scales=v_scl[:],
                in_=blk_t[("vg", blk)][:].rearrange("p w c t -> p (w c t)"),
            )
            blk_t[("v_codes", blk)] = v_codes
            blk_t[("v_scl", blk)] = v_scl

        def add_mask(n, j):
            w = 2 * (n // 2 // NBD) + n % 2
            s_ps = ps_s.tile([P, N], F32, name="s_ps")
            chunk[("s", n, j)] = s_ps
            for t in range(4):
                nc.tensor.matmul(
                    out=s_ps[:, t * P:(t + 1) * P],
                    lhsT=mask_t[:, w, t, j * P:(j + 1) * P],
                    rhs=ident_f[:],
                    is_transpose=True,
                    start=(t == 0),
                    stop=False,
                )

        def add_qk(n, j):
            blk, vw = n // 2, n % 2
            nc.tensor.matmul(
                out=chunk[("s", n, j)][:],
                lhsT=blk_t[("q_win", blk)][:, vw, j * P:(j + 1) * P],
                rhs=blk_t[("k_raw", blk)][:].rearrange("c (h v x) -> c h v x", h=16, v=2)[:, :, vw, :],
                start=False,
                stop=True,
            )

        def row_max(n, j):
            w = 2 * (n // 2 // NBD) + n % 2
            src = chunk[("s", n, j)]
            nb = small.tile([P, 1], F32, name="nb")
            if j in DVE_MASK:
                s_sb = spool.tile([P, N], F32, name="s_sb")
                nc.vector.scalar_tensor_tensor(out=s_sb[:], in0=src[:], scalar=SCALE, in1=blk_t[("m", w)][:, j, :],
                                               op0=ALU.mult, op1=ALU.add)
                chunk[("s", n, j)] = s_sb
                nc.vector.tensor_reduce(out=nb[:], in_=s_sb[:], axis=AX.X, op=ALU.max, negate=True)
            elif FUSED_MAX:
                s_neg = spool.tile([P, N], F32, name="s_neg")
                nc.vector.tensor_scalar(out=s_neg[:], in0=src[:], scalar1=-SCALE, scalar2=None, op0=ALU.mult,
                                        op1=ALU.min, accum_out=nb[:])
                chunk[("s", n, j)] = s_neg
            else:
                nm = small.tile([P, 1], F32, name="nm")
                nc.vector.tensor_reduce(out=nm[:], in_=src[:], axis=AX.X, op=ALU.max, negate=True)
                nc.vector.tensor_scalar_mul(out=nb[:], in0=nm[:], scalar1=SCALE)
            chunk[("nb", n, j)] = nb[:]

        def exps(n, half):
            if half == 0 and n % 2 == 0:
                blk_t[("rs", n // 2)] = small.tile([P, 8], F32, name="rs")
            for i in range(2):
                j = 2 * half + i
                e_sb = epool.tile([P, N], BF16, name="e_sb")
                nc.scalar.activation(
                    out=e_sb[:],
                    in_=chunk[("s", n, j)][:],
                    func=AF.Exp,
                    bias=chunk[("nb", n, j)],
                    scale=(1.0 if j in DVE_MASK else -1.0),
                    accum_out=blk_t[("rs", n // 2)][:, 4 * (n % 2) + j:4 * (n % 2) + j + 1],
                )
                chunk[("e", n, j)] = e_sb

        def e_transposes(n, half):
            et = ps_t.tile([P, 2, 256], F32, name="et", tag="tr")
            for i in range(2):
                e_sb = chunk[("e", n, 2 * half + i)]
                for u in range(2):
                    nc.tensor.transpose(et[:, u, i * P:(i + 1) * P], e_sb[:].bitcast(F32)[:, u * P:(u + 1) * P],
                                        ident_f[:])
            unit[("et", n, half)] = et

        def regroup(n, half):
            if half == 0:
                unit[("g", n)] = gpool.tile([P, N, 4], BF16, name="grp", align_bytes=64)
            nc.scalar.copy(
                out=unit[("g", n)][:, 256 * half:256 * half + 256, :].bitcast(F32),
                in_=unit[("et", n, half)][:].rearrange("p u q -> p q u"),
            )

        def quantise_e(n, js):
            if js[0] == 0:
                unit[("codes", n)] = gpool.tile([P, N], U32, name="codes", align_bytes=64)
                unit[("scl", n)] = gpool.tile([P, N], U8, name="scl", align_bytes=64)
            lo, hi = js[0] * P, (js[-1] + 1) * P
            nc.vector.quantize_mx(
                out=unit[("codes", n)][:, lo:hi].bitcast(FP8X4),
                scales=unit[("scl", n)][:, lo:hi],
                in_=unit[("g", n)][:, lo:hi, :].rearrange("p q t -> p (q t)"),
            )

        def mx_passes(n, js, spare=False):
            blk, vw = n // 2, n % 2
            if spare:
                o_ps = ps_s.tile([P, 4, P], F32, name="o_ps", tag="s_ps")
            else:
                o_ps = ps_o.tile([P, 4, P], F32, name="o_ps")
            for j in js:
                nc.tensor.matmul_mx(
                    out=o_ps[:, j, :],
                    lhsT=unit[("codes", n)][:, j * P:(j + 1) * P].bitcast(FP8X4),
                    lhsT_scale=unit[("scl", n)][:, j * P:(j + 1) * P],
                    rhs=blk_t[("v_codes", blk)][:, vw * P:(vw + 1) * P].bitcast(FP8X4),
                    rhs_scale=blk_t[("v_scl", blk)][:, vw * P:(vw + 1) * P],
                    start=True,
                    stop=True,
                )
            unit[("o_ps", n, js[0])] = o_ps

        def normalise(n, js):
            blk, vw = n // 2, n % 2
            if vw == 0:
                rinv = small.tile([P, 8], F32, name="rinv")
                nc.vector.reciprocal(out=rinv[:], in_=blk_t[("rs", blk)][:])
                blk_t[("rinv", blk)] = rinv
            lo, hi = js[0], js[-1] + 1
            o_sb = opool.tile([P, 4, P], F32, name="o_sb")
            nc.vector.tensor_tensor(
                out=o_sb[:, lo:hi, :],
                in0=unit[("o_ps", n, lo)][:, lo:hi, :],
                in1=blk_t[("rinv", blk)][:, 4 * vw + lo:4 * vw + hi].unsqueeze(2).to_broadcast([P, hi - lo, P]),
                op=ALU.mult,
            )
            unit[("o_sb", n, lo)] = o_sb

        def o_transposes(n, js, spare=False):
            if spare:
                ot = ps_s.tile([P, N], F32, name="ot", tag="s_ps")
            else:
                ot = ps_o.tile([P, N], F32, name="ot")
            for j in js:
                nc.tensor.transpose(ot[:, j * P:(j + 1) * P], unit[("o_sb", n, js[0])][:, j, :], ident_f[:])
            unit[("ot", n, js[0])] = ot

        def o_out(n, js, on_scalar):
            blk, vw = n // 2, n % 2
            if vw == 0:
                blk_t[("out", blk)] = opool.tile([P, HPIX], F32, name="out_sb")
            out_sb = blk_t[("out", blk)]
            h0, h1 = 4 * js[0], 4 * (js[-1] + 1)
            dst = out_sb[:].rearrange("c (h v x) -> c h v x", h=16, v=2)[:, h0:h1, vw, :]
            src = unit[("ot", n, js[0])][:, js[0] * P:(js[-1] + 1) * P].rearrange("c (h x) -> c h x", x=32)
            if on_scalar:
                nc.scalar.copy(out=dst, in_=src)
            else:
                nc.vector.tensor_copy(out=dst, in_=src)
            if vw == 1 and js[-1] == 3:
                nc.sync.dma_start(out=out_v[blk // NBD, blk % NBD], in_=out_sb[:])

        def ok(n):
            return 0 <= n < NUNITS

        warm = const.tile([P, 1], F32, name="warm")
        nc.vector.memset(warm[:], 0.0)
        nc.scalar.activation(out=warm[:], in_=warm[:], func=AF.Exp)

        load_mask(0)
        load_one("q", 0, (0,))
        load_one("k", 0)
        load_one("q", 0, (1,))
        load_mask(1)
        load_one("v", 0)
        load_blk(1)
        load_blk(2)
        load_mask(2)
        load_mask(3)
        for half in range(2):
            mask_transposes(0, half)
            mask_scale(0, half, half == 0)
        to_windows("q", 0)

        for m in range(NUNITS):
            blk, vw = m // 2, m % 2
            nxt = blk + 1
            late_mask = {4: 2, 6: 3}.get(m)
            if vw == 0 and 1 <= blk and blk + 2 < NBLK:
                load_blk(blk + 2)
            if ok(m):
                add_mask(m, 0)
                add_qk(m, 0)
            if ok(m - 1):
                e_transposes(m - 1, 0)
                regroup(m - 1, 0)
            if vw == 0 and 1 <= blk < NBLK:
                v_regroup(blk, VE_ON_ACT)
            if ok(m):
                add_mask(m, 1)
                add_qk(m, 1)
                add_mask(m, 2)
                add_mask(m, 3)
                add_qk(m, 2)
            if ok(m - 3):
                mx_passes(m - 3, ALL)
            if ok(m):
                add_qk(m, 3)
            if ok(m - 1):
                e_transposes(m - 1, 1)
            if ok(m - 4):
                o_transposes(m - 4, ALL)
            if m == 0:
                mask_transposes(1, 0)
            if vw == 1 and nxt < NBLK:
                v_transposes(nxt)
            if ok(m):
                row_max(m, 0)
                row_max(m, 1)
            if ok(m - 2):
                quantise_e(m - 2, ALL)
            if ok(m):
                row_max(m, 2)
            if ok(m - 3):
                normalise(m - 3, ALL)
            if ok(m):
                row_max(m, 3)
            if m == 0:
                to_windows("v", 0)
            if vw == 0 and nxt < NBLK:
                to_windows("v", nxt)
                to_windows("q", nxt)
            if vw == 0 and 1 <= blk < NBLK:
                quantise_v(blk)
            if late_mask is not None:
                mask_transposes(late_mask, 0)
                mask_scale(late_mask, 0, False)
            if ok(m):
                exps(m, 0)
            if m == 0:
                mask_scale(1, 0, True)
                mask_transposes(1, 1)
            if ok(m - 1):
                regroup(m - 1, 1)
            if late_mask is not None:
                mask_transposes(late_mask, 1)
                mask_scale(late_mask, 1, True)
            if ok(m - 4):
                o_out(m - 4, ALL, (m - 4) % 4 in OE_ON_ACT)
            if ok(m):
                exps(m, 1)
            if m == 0:
                mask_scale(1, 1, False)
                v_transposes(0)
                v_regroup(0, False)
                quantise_v(0)

        z = NUNITS - 1
        first, second = (0, 1), (2, 3)
        e_transposes(z, 0)
        regroup(z, 0)
        mx_passes(z - 2, ALL)
        e_transposes(z, 1)
        o_transposes(z - 3, ALL)
        quantise_e(z - 1, ALL)
        normalise(z - 2, ALL)
        quantise_e(z, first)
        regroup(z, 1)
        quantise_e(z, second)
        o_out(z - 3, ALL, True)
        mx_passes(z - 1, ALL, True)
        mx_passes(z, first, True)
        o_transposes(z - 2, ALL)
        o_out(z - 2, ALL, True)
        mx_passes(z, second, True)
        for n, js in ((z - 1, ALL), (z, first), (z, second)):
            normalise(n, js)
        for n, js in ((z - 1, ALL), (z, first), (z, second)):
            o_transposes(n, js, True)
            o_out(n, js, True)
